import numpy as np
import ml_dtypes


def mxq(x, axis, fmt="e4m3"):
    dtype, down = {"e4m3": (ml_dtypes.float8_e4m3fn, 7), "e5m2": (ml_dtypes.float8_e5m2, 14)}[fmt]
    v = np.moveaxis(np.asarray(x, np.float32).astype(ml_dtypes.bfloat16).astype(np.float64), axis, -1)
    blocks = v.reshape(v.shape[:-1] + (-1, 32))
    amax = np.abs(blocks).max(-1, keepdims=True)
    byte = np.maximum(np.where(amax > 0, np.frexp(amax)[1] - 1 + 127, 0) - down, 1)
    scale = np.exp2(byte - 127.0)
    codes = (blocks / scale).astype(np.float32).astype(dtype).astype(np.float64)
    return np.moveaxis((codes * scale).reshape(v.shape), -1, axis)


WIDE = False


def mx_kscale(k):
    if not WIDE:
        return np.ones(k)
    levels = np.array([10, -10, 5, -5, 0])
    a = np.random.permutation(np.resize(levels, k // 512 * 4)).reshape(k // 512, 4)
    idx = np.arange(k)
    return np.exp2(a[idx // 512, idx % 128 // 32])


BF16 = ml_dtypes.bfloat16


def bf(x):
    return np.asarray(x, np.float32).astype(BF16)


def f64(x):
    return np.asarray(x).astype(np.float64)


E2M1 = np.array([0.0, 0.5, 1.0, 1.5, 2.0, 3.0, 4.0, 6.0, -0.0, -0.5, -1.0, -1.5, -2.0, -3.0, -4.0, -6.0])


def pack_weight(w, fmt):
    k, n = w.shape
    w = f64(bf(w)).reshape(k // 32, 32, n)
    amax = np.abs(w).max(1)
    if fmt == "e4m3":
        byte = np.frexp(amax)[1] - 1 + 127 - 7
    else:
        mant, ex = np.frexp(amax / 6.0)
        byte = np.where(mant > 0.5, ex, ex - 1) + 127
    byte = np.clip(np.where(amax > 0, byte, 1), 1, 254)
    scaled = (w * np.exp2(127.0 - byte)[:, None, :]).reshape(k, n).astype(np.float32)
    by_word = np.ascontiguousarray(scaled.reshape(k // 512, 128, 4, n).transpose(0, 1, 3, 2))
    if fmt == "e4m3":
        words = by_word.astype(ml_dtypes.float8_e4m3fn).view(np.uint8)
    else:
        c = by_word.astype(ml_dtypes.float4_e2m1fn).view(np.uint8) & 0xF
        words = c[..., 0::2] | (c[..., 1::2] << 4)
    return np.ascontiguousarray(words), np.ascontiguousarray(byte.astype(np.uint8).reshape(k // 512, 16, n))


def unpack_weight(words, scales, fmt):
    g, p, n, _ = words.shape
    if fmt == "e4m3":
        vals = np.ascontiguousarray(words).view(ml_dtypes.float8_e4m3fn).astype(np.float64)
    else:
        nib = np.empty((g, p, n, 4), np.uint8)
        nib[..., 0::2] = words & 0xF
        nib[..., 1::2] = words >> 4
        vals = E2M1[nib]
    vals = vals * np.repeat(np.exp2(scales.astype(np.float64) - 127.0), 8, axis=1)[..., None]
    return vals.transpose(0, 1, 3, 2).reshape(g * 512, n)


B, S, C, H, D = 8, 1024, 256, 4, 128
E = H * D
EPS = 1e-15
FMT = "e4m3"


def setup_inputs():
    t = mx_kscale(E)
    q_feat = bf(np.maximum(np.random.standard_normal((B, H, S, D)), 0.0))
    vk = bf(np.random.standard_normal((B, H, D, D)) * np.sqrt(S) * t.reshape(H, D)[None, :, :, None])
    k_sum = bf(S * (0.11 + 0.02 * np.random.standard_normal((B, H, D))))
    wo = np.random.standard_normal((C, E)) * 6.0 / np.sqrt(E) / t[None, :]
    words, scales = pack_weight(np.ascontiguousarray(wo.T), FMT)
    bo = bf(np.random.standard_normal(C) * 0.1)
    return {"q_feat": q_feat,
            "vk": vk,
            "k_sum": k_sum,
            "Wo_words": words,
            "Wo_scales": scales,
            "bo": bo}


def reference(q_feat, vk, k_sum, Wo_words, Wo_scales, bo):
    hs = f64(vk) @ f64(q_feat).transpose(0, 1, 3, 2)
    den = (f64(q_feat) * f64(k_sum)[:, :, None, :]).sum(-1)
    hs = hs / (den[:, :, None, :] + EPS)
    a = hs.transpose(0, 3, 1, 2).reshape(B, S, E)
    return (mxq(a, 2, "e4m3") @ unpack_weight(Wo_words, Wo_scales, FMT)) + f64(bo)

@@ -1,0 +1,216 @@
+from contextlib import ExitStack
+
+import concourse.mybir as mybir
+from concourse.masks import make_identity
+
+BF16 = mybir.dt.bfloat16
+F32 = mybir.dt.float32
+I32 = mybir.dt.int32
+U32 = mybir.dt.uint32
+U8 = mybir.dt.uint8
+FP8X4 = mybir.dt.float8_e4m3fn_x4
+COPY = mybir.ActivationFunctionType.Copy
+ADD = mybir.AluOpType.add
+MULT = mybir.AluOpType.mult
+
+B, H, S, D, C = 8, 4, 1024, 128, 256
+E = H * D
+P = 128
+EPS = 1e-15
+TILES = S // P
+PAIR = 2
+PAIRS = B * TILES // PAIR
+PAIRS_PER_BATCH = TILES // PAIR
+UNIT = D + 1
+VK_PITCH = 136
+HALF_BANK = 256
+
+LAG_READ_OUT = 1
+LAG_TRANSPOSE_A = 3
+LAG_PROJECT = 4
+
+FLOPS = 2 * B * H * S * D * (D + 1) + 2 * B * S * E * C
+
+
+def tile_lineartransformerblock_pc_t_kernel(tc, q_feat, vk, k_sum, Wo_words, Wo_scales, bo, out):
+    nc = tc.nc
+    with ExitStack() as ctx:
+        consts = ctx.enter_context(tc.tile_pool(name="consts", bufs=1))
+        q_pool = ctx.enter_context(tc.tile_pool(name="q_pool", bufs=B))
+        vk_pool = ctx.enter_context(tc.tile_pool(name="vk_pool", bufs=B))
+        work = ctx.enter_context(tc.tile_pool(name="work", bufs=3))
+        out_pool = ctx.enter_context(tc.tile_pool(name="out_pool", bufs=4))
+        ps_one = ctx.enter_context(tc.psum_pool(name="ps_one", bufs=1))
+        ps_hs_pool = ctx.enter_context(tc.psum_pool(name="ps_hs_pool", bufs=2 * PAIR))
+        ctx.enter_context(tc.manual_schedule())
+
+        ident_bf = consts.tile([P, P], BF16)
+        make_identity(nc, ident_bf[:])
+        ident_f32 = consts.tile([P, P], F32)
+        make_identity(nc, ident_f32[:])
+        perm_bf = consts.tile([P, P], BF16)
+        nc.vector.tensor_copy(
+            out=perm_bf[:].rearrange("p (u j e) -> p u j e", u=2, e=2),
+            in_=ident_bf[:].rearrange("p (j u e) -> p u j e", u=2, e=2),
+        )
+        ks_rows = consts.tile([P, P], BF16)
+        nc.vector.memset(ks_rows[:], 0.0)
+        w_scales = consts.tile([P, C], U8, align_bytes=64)
+        nc.vector.memset(w_scales[:].bitcast(I32), 0)
+
+        vk_rows = []
+        q_rows = []
+        for b in range(B):
+            vk_b = vk_pool.tile([P, H, D], BF16, name="vk_b")
+            nc.sync.dma_start(out=vk_b[:], in_=vk[b].rearrange("h n d -> n h d"))
+            vk_rows.append(vk_b)
+            if b == 0:
+                nc.sync.dma_start(out=ks_rows[0 : B * H, :], in_=k_sum.rearrange("b h d -> (b h) d"))
+            q_b = q_pool.tile([P, H, TILES, D], BF16, name="q_b")
+            nc.sync.dma_start(
+                out=q_b[:].rearrange("p h i d -> p h (i d)"),
+                in_=q_feat[b].rearrange("h (p i) d -> p h (i d)", i=TILES),
+            )
+            q_rows.append(q_b)
+            if b == 0:
+                w_codes = consts.tile([P, 4 * C], U8, align_bytes=64)
+                nc.sync.dma_start(
+                    out=w_codes[:].bitcast(I32),
+                    in_=Wo_words[0].rearrange("p n t -> p (n t)").bitcast(I32),
+                )
+                for quad in range(4):
+                    nc.sync.dma_start(
+                        out=w_scales[32 * quad : 32 * quad + 4, :].bitcast(I32),
+                        in_=Wo_scales[0, 4 * quad : 4 * quad + 4, :].bitcast(I32),
+                    )
+                bias = consts.tile([P, C], BF16)
+                nc.sync.dma_start(out=bias[:], in_=bo.partition_broadcast(P))
+
+        vk_t = consts.tile([P, B * H, VK_PITCH], BF16)
+
+        def transpose_k_sum():
+            ps_ks = ps_one.tile([P, H, P], BF16, tag="ps_vk")
+            nc.tensor.transpose(ps_ks[:, 0, :], ks_rows[:], ident_bf[:])
+            nc.vector.tensor_copy(out=vk_t[:, :, D], in_=ps_ks[:, 0, 0 : B * H])
+
+        def transpose_vk(b):
+            ps_vk = ps_one.tile([P, H, P], BF16, tag="ps_vk")
+            for h in range(H):
+                nc.tensor.transpose(ps_vk[:, h, :], vk_rows[b][:, h, :], perm_bf[:])
+            nc.vector.tensor_copy(out=vk_t[:, H * b : H * b + H, 0:D], in_=ps_vk[:])
+
+        q_t = {}
+        a_rows = {}
+        a_codes = {}
+        a_scales = {}
+        a_words = {}
+
+        def transpose_q(k):
+            b, g = divmod(k, PAIRS_PER_BATCH)
+            ps_q = ps_one.tile([P, PAIR, H, P], BF16, tag="ps_q")
+            for x in range(PAIR):
+                for h in range(H):
+                    nc.tensor.transpose(ps_q[:, x, h, :], q_rows[b][:, h, PAIR * g + x, :], ident_bf[:])
+            q_t[k] = work.tile([P, PAIR, H, P], BF16, name="q_t")
+            nc.scalar.copy(out=q_t[k][:], in_=ps_q[:])
+
+        def read_out(k):
+            b = k // PAIRS_PER_BATCH
+            banks = []
+            for x in range(PAIR):
+                for hp in range(H // 2):
+                    ps_hs = ps_hs_pool.tile([P, 2, HALF_BANK], F32, name="ps_hs")
+                    for y in range(2):
+                        h = 2 * hp + y
+                        nc.tensor.matmul(
+                            out=ps_hs[:, y, 0:UNIT],
+                            lhsT=q_t[k][:, x, h, :],
+                            rhs=vk_t[:, H * b + h, 0:UNIT],
+                            start=True,
+                            stop=True,
+                        )
+                    banks.append(ps_hs)
+            den = work.tile([P, PAIR * H], F32, name="den")
+            for i, ps_hs in enumerate(banks):
+                nc.vector.tensor_scalar_add(out=den[:, 2 * i : 2 * i + 2], in0=ps_hs[:, :, D], scalar1=EPS)
+            rden = work.tile([P, PAIR * H], F32, name="rden")
+            nc.vector.reciprocal(out=rden[:], in_=den[:])
+            a_rows[k] = work.tile([P, PAIR, 2, E // 2], BF16, name="a_rows")
+            for x in range(PAIR):
+                for hp in range(H // 2):
+                    i = (H // 2) * x + hp
+                    ps_hs = banks[i]
+                    if hp == 0:
+                        for y in range(2):
+                            h = 2 * hp + y
+                            nc.scalar.activation(
+                                out=a_rows[k][:, x, :, 64 * h : 64 * h + 64],
+                                in_=ps_hs[:, y, 0:D].rearrange("p (u w) -> p u w", u=2),
+                                func=COPY,
+                                scale=rden[:, 2 * i + y : 2 * i + y + 1],
+                            )
+                    else:
+                        nc.vector.tensor_tensor(
+                            out=a_rows[k][:, x, :, D * hp : D * hp + D].rearrange("p u (y w) -> p y u w", y=2),
+                            in0=ps_hs[:, :, 0:D].rearrange("p y (u w) -> p y u w", u=2),
+                            in1=rden[:, 2 * i : 2 * i + 2].unsqueeze(2).unsqueeze(3).to_broadcast([P, 2, 2, 64]),
+                            op=MULT,
+                        )
+
+        def transpose_a(k):
+            ps_a = ps_one.tile([P, PAIR, 2, P], F32, tag="ps_a")
+            for x in range(PAIR):
+                for u in range(2):
+                    nc.tensor.transpose(ps_a[:, x, u, :], a_rows[k][:, x, u, :].bitcast(F32), ident_f32[:])
+            a_words[k] = work.tile([P, PAIR, P, 2], F32, name="a_words", align_bytes=64)
+            nc.scalar.copy(out=a_words[k][:], in_=ps_a[:].rearrange("p x u s -> p x s u"))
+
+        def quantise_a(k):
+            a_codes[k] = work.tile([P, PAIR * P], U32, name="a_codes", align_bytes=64)
+            a_scales[k] = work.tile([P, PAIR * P], U8, name="a_scales", align_bytes=64)
+            nc.vector.quantize_mx(
+                out=a_codes[k][:].bitcast(FP8X4),
+                scales=a_scales[k][:],
+                in_=a_words[k][:].rearrange("p x s u -> p (x s u)").bitcast(BF16),
+            )
+
+        def project(k):
+            b, g = divmod(k, PAIRS_PER_BATCH)
+            ps_o = ps_one.tile([P, PAIR, C], F32, tag="ps_o")
+            for x in range(PAIR):
+                nc.tensor.matmul_mx(
+                    out=ps_o[:, x, :],
+                    lhsT=a_codes[k][:, P * x : P * x + P].bitcast(FP8X4),
+                    lhsT_scale=a_scales[k][:, P * x : P * x + P],
+                    rhs=w_codes[:].bitcast(FP8X4),
+                    rhs_scale=w_scales[:],
+                    start=True,
+                    stop=True,
+                )
+            o_rows = out_pool.tile([P, PAIR, C], F32, name="o_rows")
+            nc.vector.tensor_tensor(
+                out=o_rows[:],
+                in0=ps_o[:],
+                in1=bias[:].unsqueeze(1).to_broadcast([P, PAIR, C]),
+                op=ADD,
+            )
+            nc.sync.dma_start(
+                out=out[b].rearrange("(p i) c -> p i c", i=TILES)[:, PAIR * g : PAIR * g + PAIR, :],
+                in_=o_rows[:],
+            )
+
+        transpose_k_sum()
+        transpose_vk(0)
+        for r in range(PAIRS + LAG_PROJECT):
+            if r < PAIRS:
+                transpose_q(r)
+            if 0 <= r - LAG_TRANSPOSE_A < PAIRS:
+                transpose_a(r - LAG_TRANSPOSE_A)
+            if r % PAIRS_PER_BATCH == 0 and r // PAIRS_PER_BATCH + 1 < B:
+                transpose_vk(r // PAIRS_PER_BATCH + 1)
+            if 0 <= r - LAG_READ_OUT < PAIRS:
+                read_out(r - LAG_READ_OUT)
+            if 0 <= r - LAG_TRANSPOSE_A < PAIRS:
+                quantise_a(r - LAG_TRANSPOSE_A)
+            if 0 <= r - LAG_PROJECT < PAIRS:
+                project(r - LAG_PROJECT)

@@ -21,13 +21,12 @@ TILES = S // P
 PAIR = 2
 PAIRS = B * TILES // PAIR
 PAIRS_PER_BATCH = TILES // PAIR
-UNIT = D + 1
-VK_PITCH = 136
-HALF_BANK = 256
 
 LAG_READ_OUT = 1
 LAG_TRANSPOSE_A = 3
 LAG_PROJECT = 4
+LAG_STORE = 5
+VK_PER_ROUND = 2
 
 FLOPS = 2 * B * H * S * D * (D + 1) + 2 * B * S * E * C
 
@@ -37,7 +36,6 @@ def tile_lineartransformerblock_pc_t_kernel(tc, q_feat, vk, k_sum, Wo_words, Wo_
     with ExitStack() as ctx:
         consts = ctx.enter_context(tc.tile_pool(name="consts", bufs=1))
         q_pool = ctx.enter_context(tc.tile_pool(name="q_pool", bufs=B))
-        vk_pool = ctx.enter_context(tc.tile_pool(name="vk_pool", bufs=B))
         work = ctx.enter_context(tc.tile_pool(name="work", bufs=3))
         out_pool = ctx.enter_context(tc.tile_pool(name="out_pool", bufs=4))
         ps_one = ctx.enter_context(tc.psum_pool(name="ps_one", bufs=1))
@@ -58,14 +56,12 @@ def tile_lineartransformerblock_pc_t_kernel(tc, q_feat, vk, k_sum, Wo_words, Wo_
         w_scales = consts.tile([P, C], U8, align_bytes=64)
         nc.vector.memset(w_scales[:].bitcast(I32), 0)
 
-        vk_rows = []
+        vk_rows = consts.tile([P, B * H, D], BF16)
+        vk_view = vk.rearrange("b h n d -> n (b h) d")
+        nc.sync.dma_start(out=vk_rows[:, 0:H, :], in_=vk_view[:, 0:H, :])
+        nc.sync.dma_start(out=ks_rows[0 : B * H, :], in_=k_sum.rearrange("b h d -> (b h) d"))
         q_rows = []
         for b in range(B):
-            vk_b = vk_pool.tile([P, H, D], BF16, name="vk_b")
-            nc.sync.dma_start(out=vk_b[:], in_=vk[b].rearrange("h n d -> n h d"))
-            vk_rows.append(vk_b)
-            if b == 0:
-                nc.sync.dma_start(out=ks_rows[0 : B * H, :], in_=k_sum.rearrange("b h d -> (b h) d"))
             q_b = q_pool.tile([P, H, TILES, D], BF16, name="q_b")
             nc.sync.dma_start(
                 out=q_b[:].rearrange("p h i d -> p h (i d)"),
@@ -85,25 +81,29 @@ def tile_lineartransformerblock_pc_t_kernel(tc, q_feat, vk, k_sum, Wo_words, Wo_
                     )
                 bias = consts.tile([P, C], BF16)
                 nc.sync.dma_start(out=bias[:], in_=bo.partition_broadcast(P))
+                nc.sync.dma_start(out=vk_rows[:, H:, :], in_=vk_view[:, H:, :])
 
-        vk_t = consts.tile([P, B * H, VK_PITCH], BF16)
+        vk_t = consts.tile([P, B * H, D], BF16)
+        ks_t = consts.tile([P, B * H], BF16)
 
         def transpose_k_sum():
-            ps_ks = ps_one.tile([P, H, P], BF16, tag="ps_vk")
+            ps_ks = ps_one.tile([P, H, P], BF16, tag="ps_o")
             nc.tensor.transpose(ps_ks[:, 0, :], ks_rows[:], ident_bf[:])
-            nc.vector.tensor_copy(out=vk_t[:, :, D], in_=ps_ks[:, 0, 0 : B * H])
+            nc.vector.tensor_copy(out=ks_t[:], in_=ps_ks[:, 0, 0 : B * H])
 
         def transpose_vk(b):
-            ps_vk = ps_one.tile([P, H, P], BF16, tag="ps_vk")
+            ps_vk = ps_one.tile([P, H, P], BF16, tag="ps_o")
             for h in range(H):
-                nc.tensor.transpose(ps_vk[:, h, :], vk_rows[b][:, h, :], perm_bf[:])
-            nc.vector.tensor_copy(out=vk_t[:, H * b : H * b + H, 0:D], in_=ps_vk[:])
+                nc.tensor.transpose(ps_vk[:, h, :], vk_rows[:, H * b + h, :], perm_bf[:])
+            nc.vector.tensor_copy(out=vk_t[:, H * b : H * b + H, :], in_=ps_vk[:])
 
         q_t = {}
+        rden = {}
         a_rows = {}
+        a_words = {}
         a_codes = {}
         a_scales = {}
-        a_words = {}
+        ps_out = {}
 
         def transpose_q(k):
             b, g = divmod(k, PAIRS_PER_BATCH)
@@ -114,48 +114,51 @@ def tile_lineartransformerblock_pc_t_kernel(tc, q_feat, vk, k_sum, Wo_words, Wo_
             q_t[k] = work.tile([P, PAIR, H, P], BF16, name="q_t")
             nc.scalar.copy(out=q_t[k][:], in_=ps_q[:])
 
+        def denominators(k):
+            b = k // PAIRS_PER_BATCH
+            ps_den = ps_one.tile([P, PAIR, H], F32, tag="ps_den")
+            for x in range(PAIR):
+                for h in range(H):
+                    nc.tensor.matmul(
+                        out=ps_den[:, x, h : h + 1],
+                        lhsT=q_t[k][:, x, h, :],
+                        rhs=ks_t[:, H * b + h : H * b + h + 1],
+                        start=True,
+                        stop=True,
+                    )
+            den = work.tile([P, PAIR, H], F32, name="den")
+            nc.vector.tensor_scalar_add(out=den[:], in0=ps_den[:], scalar1=EPS)
+            rden[k] = work.tile([P, PAIR, H], F32, name="rden")
+            nc.vector.reciprocal(out=rden[k][:], in_=den[:])
+
         def read_out(k):
             b = k // PAIRS_PER_BATCH
+            a_rows[k] = work.tile([P, PAIR, 2, E // 2], BF16, name="a_rows")
             banks = []
             for x in range(PAIR):
-                for hp in range(H // 2):
-                    ps_hs = ps_hs_pool.tile([P, 2, HALF_BANK], F32, name="ps_hs")
-                    for y in range(2):
-                        h = 2 * hp + y
-                        nc.tensor.matmul(
-                            out=ps_hs[:, y, 0:UNIT],
-                            lhsT=q_t[k][:, x, h, :],
-                            rhs=vk_t[:, H * b + h, 0:UNIT],
-                            start=True,
-                            stop=True,
-                        )
-                    banks.append(ps_hs)
-            den = work.tile([P, PAIR * H], F32, name="den")
-            for i, ps_hs in enumerate(banks):
-                nc.vector.tensor_scalar_add(out=den[:, 2 * i : 2 * i + 2], in0=ps_hs[:, :, D], scalar1=EPS)
-            rden = work.tile([P, PAIR * H], F32, name="rden")
-            nc.vector.reciprocal(out=rden[:], in_=den[:])
-            a_rows[k] = work.tile([P, PAIR, 2, E // 2], BF16, name="a_rows")
-            for x in range(PAIR):
-                for hp in range(H // 2):
-                    i = (H // 2) * x + hp
-                    ps_hs = banks[i]
-                    if hp == 0:
-                        for y in range(2):
-                            h = 2 * hp + y
-                            nc.scalar.activation(
-                                out=a_rows[k][:, x, :, 64 * h : 64 * h + 64],
-                                in_=ps_hs[:, y, 0:D].rearrange("p (u w) -> p u w", u=2),
-                                func=COPY,
-                                scale=rden[:, 2 * i + y : 2 * i + y + 1],
-                            )
-                    else:
-                        nc.vector.tensor_tensor(
-                            out=a_rows[k][:, x, :, D * hp : D * hp + D].rearrange("p u (y w) -> p y u w", y=2),
-                            in0=ps_hs[:, :, 0:D].rearrange("p y (u w) -> p y u w", u=2),
-                            in1=rden[:, 2 * i : 2 * i + 2].unsqueeze(2).unsqueeze(3).to_broadcast([P, 2, 2, 64]),
-                            op=MULT,
-                        )
+                ps_hs = ps_hs_pool.tile([P, H, D], F32, name="ps_hs")
+                for h in range(H):
+                    nc.tensor.matmul(
+                        out=ps_hs[:, h, :],
+                        lhsT=q_t[k][:, x, h, :],
+                        rhs=vk_t[:, H * b + h, :],
+                        start=True,
+                        stop=True,
+                    )
+                banks.append(ps_hs)
+            for h in range(H):
+                nc.scalar.activation(
+                    out=a_rows[k][:, 0, :, 64 * h : 64 * h + 64],
+                    in_=banks[0][:, h, :].rearrange("p (u w) -> p u w", u=2),
+                    func=COPY,
+                    scale=rden[k][:, 0, h : h + 1],
+                )
+            nc.vector.tensor_tensor(
+                out=a_rows[k][:, 1, :, :].rearrange("p u (h w) -> p h u w", h=H),
+                in0=banks[1][:].rearrange("p h (u w) -> p h u w", u=2),
+                in1=rden[k][:, 1, :].unsqueeze(2).unsqueeze(3).to_broadcast([P, H, 2, 64]),
+                op=MULT,
+            )
 
         def transpose_a(k):
             ps_a = ps_one.tile([P, PAIR, 2, P], F32, tag="ps_a")
@@ -175,11 +178,10 @@ def tile_lineartransformerblock_pc_t_kernel(tc, q_feat, vk, k_sum, Wo_words, Wo_
             )
 
         def project(k):
-            b, g = divmod(k, PAIRS_PER_BATCH)
-            ps_o = ps_one.tile([P, PAIR, C], F32, tag="ps_o")
+            ps_out[k] = ps_one.tile([P, PAIR, C], F32, tag="ps_o", name="ps_o")
             for x in range(PAIR):
                 nc.tensor.matmul_mx(
-                    out=ps_o[:, x, :],
+                    out=ps_out[k][:, x, :],
                     lhsT=a_codes[k][:, P * x : P * x + P].bitcast(FP8X4),
                     lhsT_scale=a_scales[k][:, P * x : P * x + P],
                     rhs=w_codes[:].bitcast(FP8X4),
@@ -187,10 +189,13 @@ def tile_lineartransformerblock_pc_t_kernel(tc, q_feat, vk, k_sum, Wo_words, Wo_
                     start=True,
                     stop=True,
                 )
+
+        def add_bias_and_store(k):
+            b, g = divmod(k, PAIRS_PER_BATCH)
             o_rows = out_pool.tile([P, PAIR, C], F32, name="o_rows")
             nc.vector.tensor_tensor(
                 out=o_rows[:],
-                in0=ps_o[:],
+                in0=ps_out[k][:],
                 in1=bias[:].unsqueeze(1).to_broadcast([P, PAIR, C]),
                 op=ADD,
             )
@@ -201,16 +206,20 @@ def tile_lineartransformerblock_pc_t_kernel(tc, q_feat, vk, k_sum, Wo_words, Wo_
 
         transpose_k_sum()
         transpose_vk(0)
-        for r in range(PAIRS + LAG_PROJECT):
+        for r in range(PAIRS + LAG_STORE):
+            if 0 <= r - LAG_STORE < PAIRS:
+                add_bias_and_store(r - LAG_STORE)
+            if 0 <= r - LAG_PROJECT < PAIRS:
+                quantise_a(r - LAG_PROJECT)
             if r < PAIRS:
                 transpose_q(r)
             if 0 <= r - LAG_TRANSPOSE_A < PAIRS:
                 transpose_a(r - LAG_TRANSPOSE_A)
-            if r % PAIRS_PER_BATCH == 0 and r // PAIRS_PER_BATCH + 1 < B:
-                transpose_vk(r // PAIRS_PER_BATCH + 1)
+            if r < LAG_PROJECT:
+                for b in range(1 + VK_PER_ROUND * r, min(B, 1 + VK_PER_ROUND * (r + 1))):
+                    transpose_vk(b)
             if 0 <= r - LAG_READ_OUT < PAIRS:
+                denominators(r - LAG_READ_OUT)
                 read_out(r - LAG_READ_OUT)
-            if 0 <= r - LAG_TRANSPOSE_A < PAIRS:
-                quantise_a(r - LAG_TRANSPOSE_A)
             if 0 <= r - LAG_PROJECT < PAIRS:
                 project(r - LAG_PROJECT)

@@ -9,7 +9,6 @@ I32 = mybir.dt.int32
 U32 = mybir.dt.uint32
 U8 = mybir.dt.uint8
 FP8X4 = mybir.dt.float8_e4m3fn_x4
-COPY = mybir.ActivationFunctionType.Copy
 ADD = mybir.AluOpType.add
 MULT = mybir.AluOpType.mult
 
@@ -79,8 +78,10 @@ def tile_lineartransformerblock_pc_t_kernel(tc, q_feat, vk, k_sum, Wo_words, Wo_
                         out=w_scales[32 * quad : 32 * quad + 4, :].bitcast(I32),
                         in_=Wo_scales[0, 4 * quad : 4 * quad + 4, :].bitcast(I32),
                     )
-                bias = consts.tile([P, C], BF16)
-                nc.sync.dma_start(out=bias[:], in_=bo.partition_broadcast(P))
+                bias_bf = consts.tile([P, C], BF16)
+                nc.sync.dma_start(out=bias_bf[:], in_=bo.partition_broadcast(P))
+                bias = consts.tile([P, C], F32)
+                nc.gpsimd.tensor_copy(out=bias[:], in_=bias_bf[:])
                 nc.sync.dma_start(out=vk_rows[:, H:, :], in_=vk_view[:, H:, :])
 
         vk_t = consts.tile([P, B * H, D], BF16)
@@ -112,7 +113,10 @@ def tile_lineartransformerblock_pc_t_kernel(tc, q_feat, vk, k_sum, Wo_words, Wo_
                 for h in range(H):
                     nc.tensor.transpose(ps_q[:, x, h, :], q_rows[b][:, h, PAIR * g + x, :], ident_bf[:])
             q_t[k] = work.tile([P, PAIR, H, P], BF16, name="q_t")
-            nc.scalar.copy(out=q_t[k][:], in_=ps_q[:])
+            if k % 2 == 0:
+                nc.scalar.copy(out=q_t[k][:], in_=ps_q[:])
+            else:
+                nc.vector.tensor_copy(out=q_t[k][:], in_=ps_q[:])
 
         def denominators(k):
             b = k // PAIRS_PER_BATCH
@@ -146,19 +150,13 @@ def tile_lineartransformerblock_pc_t_kernel(tc, q_feat, vk, k_sum, Wo_words, Wo_
                         stop=True,
                     )
                 banks.append(ps_hs)
-            for h in range(H):
-                nc.scalar.activation(
-                    out=a_rows[k][:, 0, :, 64 * h : 64 * h + 64],
-                    in_=banks[0][:, h, :].rearrange("p (u w) -> p u w", u=2),
-                    func=COPY,
-                    scale=rden[k][:, 0, h : h + 1],
+            for x in range(PAIR):
+                nc.vector.tensor_tensor(
+                    out=a_rows[k][:, x, :, :].rearrange("p u (h w) -> p h u w", h=H),
+                    in0=banks[x][:].rearrange("p h (u w) -> p h u w", u=2),
+                    in1=rden[k][:, x, :].unsqueeze(2).unsqueeze(3).to_broadcast([P, H, 2, 64]),
+                    op=MULT,
                 )
-            nc.vector.tensor_tensor(
-                out=a_rows[k][:, 1, :, :].rearrange("p u (h w) -> p h u w", h=H),
-                in0=banks[1][:].rearrange("p h (u w) -> p h u w", u=2),
-                in1=rden[k][:, 1, :].unsqueeze(2).unsqueeze(3).to_broadcast([P, H, 2, 64]),
-                op=MULT,
-            )
 
         def transpose_a(k):
             ps_a = ps_one.tile([P, PAIR, 2, P], F32, tag="ps_a")
@@ -192,10 +190,12 @@ def tile_lineartransformerblock_pc_t_kernel(tc, q_feat, vk, k_sum, Wo_words, Wo_
 
         def add_bias_and_store(k):
             b, g = divmod(k, PAIRS_PER_BATCH)
+            o_sums = out_pool.tile([P, PAIR, C], F32, name="o_sums")
+            nc.scalar.copy(out=o_sums[:], in_=ps_out[k][:])
             o_rows = out_pool.tile([P, PAIR, C], F32, name="o_rows")
-            nc.vector.tensor_tensor(
+            nc.gpsimd.tensor_tensor(
                 out=o_rows[:],
-                in0=ps_out[k][:],
+                in0=o_sums[:],
                 in1=bias[:].unsqueeze(1).to_broadcast([P, PAIR, C]),
                 op=ADD,
             )

@@ -9,8 +9,8 @@ I32 = mybir.dt.int32
 U32 = mybir.dt.uint32
 U8 = mybir.dt.uint8
 FP8X4 = mybir.dt.float8_e4m3fn_x4
+COPY = mybir.ActivationFunctionType.Copy
 ADD = mybir.AluOpType.add
-MULT = mybir.AluOpType.mult
 
 B, H, S, D, C = 8, 4, 1024, 128, 256
 E = H * D
@@ -21,10 +21,11 @@ PAIR = 2
 PAIRS = B * TILES // PAIR
 PAIRS_PER_BATCH = TILES // PAIR
 
-LAG_READ_OUT = 1
-LAG_TRANSPOSE_A = 3
-LAG_PROJECT = 4
-LAG_STORE = 5
+LAG_DENOMINATORS = 1
+LAG_READ_OUT = 2
+LAG_TRANSPOSE_A = 4
+LAG_QUANTISE = 5
+LAG_PROJECT = 6
 VK_PER_ROUND = 2
 
 FLOPS = 2 * B * H * S * D * (D + 1) + 2 * B * S * E * C
@@ -35,7 +36,7 @@ def tile_lineartransformerblock_pc_t_kernel(tc, q_feat, vk, k_sum, Wo_words, Wo_
     with ExitStack() as ctx:
         consts = ctx.enter_context(tc.tile_pool(name="consts", bufs=1))
         q_pool = ctx.enter_context(tc.tile_pool(name="q_pool", bufs=B))
-        work = ctx.enter_context(tc.tile_pool(name="work", bufs=3))
+        work = ctx.enter_context(tc.tile_pool(name="work", bufs=4))
         out_pool = ctx.enter_context(tc.tile_pool(name="out_pool", bufs=4))
         ps_one = ctx.enter_context(tc.psum_pool(name="ps_one", bufs=1))
         ps_hs_pool = ctx.enter_context(tc.psum_pool(name="ps_hs_pool", bufs=2 * PAIR))
@@ -78,10 +79,8 @@ def tile_lineartransformerblock_pc_t_kernel(tc, q_feat, vk, k_sum, Wo_words, Wo_
                         out=w_scales[32 * quad : 32 * quad + 4, :].bitcast(I32),
                         in_=Wo_scales[0, 4 * quad : 4 * quad + 4, :].bitcast(I32),
                     )
-                bias_bf = consts.tile([P, C], BF16)
-                nc.sync.dma_start(out=bias_bf[:], in_=bo.partition_broadcast(P))
-                bias = consts.tile([P, C], F32)
-                nc.gpsimd.tensor_copy(out=bias[:], in_=bias_bf[:])
+                bias = consts.tile([P, C], BF16)
+                nc.sync.dma_start(out=bias[:], in_=bo.partition_broadcast(P))
                 nc.sync.dma_start(out=vk_rows[:, H:, :], in_=vk_view[:, H:, :])
 
         vk_t = consts.tile([P, B * H, D], BF16)
@@ -113,10 +112,7 @@ def tile_lineartransformerblock_pc_t_kernel(tc, q_feat, vk, k_sum, Wo_words, Wo_
                 for h in range(H):
                     nc.tensor.transpose(ps_q[:, x, h, :], q_rows[b][:, h, PAIR * g + x, :], ident_bf[:])
             q_t[k] = work.tile([P, PAIR, H, P], BF16, name="q_t")
-            if k % 2 == 0:
-                nc.scalar.copy(out=q_t[k][:], in_=ps_q[:])
-            else:
-                nc.vector.tensor_copy(out=q_t[k][:], in_=ps_q[:])
+            nc.vector.tensor_copy(out=q_t[k][:], in_=ps_q[:])
 
         def denominators(k):
             b = k // PAIRS_PER_BATCH
@@ -151,12 +147,13 @@ def tile_lineartransformerblock_pc_t_kernel(tc, q_feat, vk, k_sum, Wo_words, Wo_
                     )
                 banks.append(ps_hs)
             for x in range(PAIR):
-                nc.vector.tensor_tensor(
-                    out=a_rows[k][:, x, :, :].rearrange("p u (h w) -> p h u w", h=H),
-                    in0=banks[x][:].rearrange("p h (u w) -> p h u w", u=2),
-                    in1=rden[k][:, x, :].unsqueeze(2).unsqueeze(3).to_broadcast([P, H, 2, 64]),
-                    op=MULT,
-                )
+                for h in range(H):
+                    nc.scalar.activation(
+                        out=a_rows[k][:, x, :, 64 * h : 64 * h + 64],
+                        in_=banks[x][:, h, :].rearrange("p (u w) -> p u w", u=2),
+                        func=COPY,
+                        scale=rden[k][:, x, h : h + 1],
+                    )
 
         def transpose_a(k):
             ps_a = ps_one.tile([P, PAIR, 2, P], F32, tag="ps_a")
@@ -190,12 +187,10 @@ def tile_lineartransformerblock_pc_t_kernel(tc, q_feat, vk, k_sum, Wo_words, Wo_
 
         def add_bias_and_store(k):
             b, g = divmod(k, PAIRS_PER_BATCH)
-            o_sums = out_pool.tile([P, PAIR, C], F32, name="o_sums")
-            nc.scalar.copy(out=o_sums[:], in_=ps_out[k][:])
             o_rows = out_pool.tile([P, PAIR, C], F32, name="o_rows")
-            nc.gpsimd.tensor_tensor(
+            nc.vector.tensor_tensor(
                 out=o_rows[:],
-                in0=o_sums[:],
+                in0=ps_out[k][:],
                 in1=bias[:].unsqueeze(1).to_broadcast([P, PAIR, C]),
                 op=ADD,
             )
@@ -206,20 +201,20 @@ def tile_lineartransformerblock_pc_t_kernel(tc, q_feat, vk, k_sum, Wo_words, Wo_
 
         transpose_k_sum()
         transpose_vk(0)
-        for r in range(PAIRS + LAG_STORE):
-            if 0 <= r - LAG_STORE < PAIRS:
-                add_bias_and_store(r - LAG_STORE)
-            if 0 <= r - LAG_PROJECT < PAIRS:
-                quantise_a(r - LAG_PROJECT)
+        for r in range(PAIRS + LAG_PROJECT):
             if r < PAIRS:
                 transpose_q(r)
             if 0 <= r - LAG_TRANSPOSE_A < PAIRS:
                 transpose_a(r - LAG_TRANSPOSE_A)
-            if r < LAG_PROJECT:
+            if r < LAG_TRANSPOSE_A:
                 for b in range(1 + VK_PER_ROUND * r, min(B, 1 + VK_PER_ROUND * (r + 1))):
                     transpose_vk(b)
+            if 0 <= r - LAG_QUANTISE < PAIRS:
+                quantise_a(r - LAG_QUANTISE)
             if 0 <= r - LAG_READ_OUT < PAIRS:
-                denominators(r - LAG_READ_OUT)
                 read_out(r - LAG_READ_OUT)
             if 0 <= r - LAG_PROJECT < PAIRS:
                 project(r - LAG_PROJECT)
+                add_bias_and_store(r - LAG_PROJECT)
+            if 0 <= r - LAG_DENOMINATORS < PAIRS:
+                denominators(r - LAG_DENOMINATORS)

@@ -38,8 +38,8 @@ def tile_lineartransformerblock_pc_t_kernel(tc, q_feat, vk, k_sum, Wo_words, Wo_
         q_pool = ctx.enter_context(tc.tile_pool(name="q_pool", bufs=B))
         work = ctx.enter_context(tc.tile_pool(name="work", bufs=4))
         out_pool = ctx.enter_context(tc.tile_pool(name="out_pool", bufs=4))
-        ps_one = ctx.enter_context(tc.psum_pool(name="ps_one", bufs=1))
-        ps_hs_pool = ctx.enter_context(tc.psum_pool(name="ps_hs_pool", bufs=2 * PAIR))
+        ps_den_pool = ctx.enter_context(tc.psum_pool(name="ps_den_pool", bufs=1))
+        psum = ctx.enter_context(tc.psum_pool(name="psum", bufs=7))
         ctx.enter_context(tc.manual_schedule())
 
         ident_bf = consts.tile([P, P], BF16)
@@ -87,12 +87,12 @@ def tile_lineartransformerblock_pc_t_kernel(tc, q_feat, vk, k_sum, Wo_words, Wo_
         ks_t = consts.tile([P, B * H], BF16)
 
         def transpose_k_sum():
-            ps_ks = ps_one.tile([P, H, P], BF16, tag="ps_o")
+            ps_ks = psum.tile([P, H, P], BF16, tag="bank")
             nc.tensor.transpose(ps_ks[:, 0, :], ks_rows[:], ident_bf[:])
             nc.vector.tensor_copy(out=ks_t[:], in_=ps_ks[:, 0, 0 : B * H])
 
         def transpose_vk(b):
-            ps_vk = ps_one.tile([P, H, P], BF16, tag="ps_o")
+            ps_vk = psum.tile([P, H, P], BF16, tag="bank")
             for h in range(H):
                 nc.tensor.transpose(ps_vk[:, h, :], vk_rows[:, H * b + h, :], perm_bf[:])
             nc.vector.tensor_copy(out=vk_t[:, H * b : H * b + H, :], in_=ps_vk[:])
@@ -107,7 +107,7 @@ def tile_lineartransformerblock_pc_t_kernel(tc, q_feat, vk, k_sum, Wo_words, Wo_
 
         def transpose_q(k):
             b, g = divmod(k, PAIRS_PER_BATCH)
-            ps_q = ps_one.tile([P, PAIR, H, P], BF16, tag="ps_q")
+            ps_q = psum.tile([P, PAIR, H, P], BF16, tag="bank")
             for x in range(PAIR):
                 for h in range(H):
                     nc.tensor.transpose(ps_q[:, x, h, :], q_rows[b][:, h, PAIR * g + x, :], ident_bf[:])
@@ -116,7 +116,7 @@ def tile_lineartransformerblock_pc_t_kernel(tc, q_feat, vk, k_sum, Wo_words, Wo_
 
         def denominators(k):
             b = k // PAIRS_PER_BATCH
-            ps_den = ps_one.tile([P, PAIR, H], F32, tag="ps_den")
+            ps_den = ps_den_pool.tile([P, PAIR, H], F32)
             for x in range(PAIR):
                 for h in range(H):
                     nc.tensor.matmul(
@@ -131,32 +131,29 @@ def tile_lineartransformerblock_pc_t_kernel(tc, q_feat, vk, k_sum, Wo_words, Wo_
             rden[k] = work.tile([P, PAIR, H], F32, name="rden")
             nc.vector.reciprocal(out=rden[k][:], in_=den[:])
 
-        def read_out(k):
+        def read_out(k, x):
             b = k // PAIRS_PER_BATCH
-            a_rows[k] = work.tile([P, PAIR, 2, E // 2], BF16, name="a_rows")
-            banks = []
-            for x in range(PAIR):
-                ps_hs = ps_hs_pool.tile([P, H, D], F32, name="ps_hs")
-                for h in range(H):
-                    nc.tensor.matmul(
-                        out=ps_hs[:, h, :],
-                        lhsT=q_t[k][:, x, h, :],
-                        rhs=vk_t[:, H * b + h, :],
-                        start=True,
-                        stop=True,
-                    )
-                banks.append(ps_hs)
-            for x in range(PAIR):
-                for h in range(H):
-                    nc.scalar.activation(
-                        out=a_rows[k][:, x, :, 64 * h : 64 * h + 64],
-                        in_=banks[x][:, h, :].rearrange("p (u w) -> p u w", u=2),
-                        func=COPY,
-                        scale=rden[k][:, x, h : h + 1],
-                    )
+            if x == 0:
+                a_rows[k] = work.tile([P, PAIR, 2, E // 2], BF16, name="a_rows")
+            ps_hs = psum.tile([P, H, D], F32, tag="bank")
+            for h in range(H):
+                nc.tensor.matmul(
+                    out=ps_hs[:, h, :],
+                    lhsT=q_t[k][:, x, h, :],
+                    rhs=vk_t[:, H * b + h, :],
+                    start=True,
+                    stop=True,
+                )
+            for h in range(H):
+                nc.scalar.activation(
+                    out=a_rows[k][:, x, :, 64 * h : 64 * h + 64],
+                    in_=ps_hs[:, h, :].rearrange("p (u w) -> p u w", u=2),
+                    func=COPY,
+                    scale=rden[k][:, x, h : h + 1],
+                )
 
         def transpose_a(k):
-            ps_a = ps_one.tile([P, PAIR, 2, P], F32, tag="ps_a")
+            ps_a = psum.tile([P, PAIR, 2, P], F32, tag="bank")
             for x in range(PAIR):
                 for u in range(2):
                     nc.tensor.transpose(ps_a[:, x, u, :], a_rows[k][:, x, u, :].bitcast(F32), ident_f32[:])
@@ -173,7 +170,7 @@ def tile_lineartransformerblock_pc_t_kernel(tc, q_feat, vk, k_sum, Wo_words, Wo_
             )
 
         def project(k):
-            ps_out[k] = ps_one.tile([P, PAIR, C], F32, tag="ps_o", name="ps_o")
+            ps_out[k] = psum.tile([P, PAIR, C], F32, tag="bank", name="ps_o")
             for x in range(PAIR):
                 nc.tensor.matmul_mx(
                     out=ps_out[k][:, x, :],
@@ -212,9 +209,11 @@ def tile_lineartransformerblock_pc_t_kernel(tc, q_feat, vk, k_sum, Wo_words, Wo_
             if 0 <= r - LAG_QUANTISE < PAIRS:
                 quantise_a(r - LAG_QUANTISE)
             if 0 <= r - LAG_READ_OUT < PAIRS:
-                read_out(r - LAG_READ_OUT)
+                read_out(r - LAG_READ_OUT, 0)
             if 0 <= r - LAG_PROJECT < PAIRS:
                 project(r - LAG_PROJECT)
                 add_bias_and_store(r - LAG_PROJECT)
+            if 0 <= r - LAG_READ_OUT < PAIRS:
+                read_out(r - LAG_READ_OUT, 1)
             if 0 <= r - LAG_DENOMINATORS < PAIRS:
                 denominators(r - LAG_DENOMINATORS)

@@ -11,6 +11,7 @@ U8 = mybir.dt.uint8
 FP8X4 = mybir.dt.float8_e4m3fn_x4
 COPY = mybir.ActivationFunctionType.Copy
 ADD = mybir.AluOpType.add
+MULT = mybir.AluOpType.mult
 
 B, H, S, D, C = 8, 4, 1024, 128, 256
 E = H * D
@@ -24,9 +25,10 @@ PAIRS_PER_BATCH = TILES // PAIR
 LAG_DENOMINATORS = 1
 LAG_READ_OUT = 2
 LAG_TRANSPOSE_A = 4
-LAG_QUANTISE = 5
+LAG_QUANTISE = 4
 LAG_PROJECT = 6
 VK_PER_ROUND = 2
+FIRST_VK_ROUND = 2
 
 FLOPS = 2 * B * H * S * D * (D + 1) + 2 * B * S * E * C
 
@@ -58,30 +60,38 @@ def tile_lineartransformerblock_pc_t_kernel(tc, q_feat, vk, k_sum, Wo_words, Wo_
 
         vk_rows = consts.tile([P, B * H, D], BF16)
         vk_view = vk.rearrange("b h n d -> n (b h) d")
-        nc.sync.dma_start(out=vk_rows[:, 0:H, :], in_=vk_view[:, 0:H, :])
-        nc.sync.dma_start(out=ks_rows[0 : B * H, :], in_=k_sum.rearrange("b h d -> (b h) d"))
         q_rows = []
         for b in range(B):
             q_b = q_pool.tile([P, H, TILES, D], BF16, name="q_b")
-            nc.sync.dma_start(
-                out=q_b[:].rearrange("p h i d -> p h (i d)"),
-                in_=q_feat[b].rearrange("h (p i) d -> p h (i d)", i=TILES),
-            )
             q_rows.append(q_b)
-            if b == 0:
-                w_codes = consts.tile([P, 4 * C], U8, align_bytes=64)
-                nc.sync.dma_start(
-                    out=w_codes[:].bitcast(I32),
-                    in_=Wo_words[0].rearrange("p n t -> p (n t)").bitcast(I32),
-                )
-                for quad in range(4):
-                    nc.sync.dma_start(
-                        out=w_scales[32 * quad : 32 * quad + 4, :].bitcast(I32),
-                        in_=Wo_scales[0, 4 * quad : 4 * quad + 4, :].bitcast(I32),
-                    )
-                bias = consts.tile([P, C], BF16)
-                nc.sync.dma_start(out=bias[:], in_=bo.partition_broadcast(P))
-                nc.sync.dma_start(out=vk_rows[:, H:, :], in_=vk_view[:, H:, :])
+
+        def load_q(b, first_tile, tiles):
+            nc.sync.dma_start(
+                out=q_rows[b][:, :, first_tile : first_tile + tiles, :],
+                in_=q_feat[b].rearrange("h (p i) d -> p h i d", i=TILES)[:, :, first_tile : first_tile + tiles, :],
+            )
+
+        load_q(0, 0, PAIR)
+        nc.sync.dma_start(out=vk_rows[:, 0:H, :], in_=vk_view[:, 0:H, :])
+        nc.sync.dma_start(out=ks_rows[0 : B * H, :], in_=k_sum.rearrange("b h d -> (b h) d"))
+        for g in range(1, PAIRS_PER_BATCH):
+            load_q(0, PAIR * g, PAIR)
+        nc.sync.dma_start(out=vk_rows[:, H:, :], in_=vk_view[:, H:, :])
+        w_codes = consts.tile([P, 4 * C], U8, align_bytes=64)
+        nc.sync.dma_start(
+            out=w_codes[:].bitcast(I32),
+            in_=Wo_words[0].rearrange("p n t -> p (n t)").bitcast(I32),
+        )
+        for quad in range(4):
+            nc.sync.dma_start(
+                out=w_scales[32 * quad : 32 * quad + 4, :].bitcast(I32),
+                in_=Wo_scales[0, 4 * quad : 4 * quad + 4, :].bitcast(I32),
+            )
+        load_q(1, 0, TILES)
+        bias = consts.tile([P, C], BF16)
+        nc.sync.dma_start(out=bias[:], in_=bo.partition_broadcast(P))
+        for b in range(2, B):
+            load_q(b, 0, TILES)
 
         vk_t = consts.tile([P, B * H, D], BF16)
         ks_t = consts.tile([P, B * H], BF16)
@@ -112,7 +122,7 @@ def tile_lineartransformerblock_pc_t_kernel(tc, q_feat, vk, k_sum, Wo_words, Wo_
                 for h in range(H):
                     nc.tensor.transpose(ps_q[:, x, h, :], q_rows[b][:, h, PAIR * g + x, :], ident_bf[:])
             q_t[k] = work.tile([P, PAIR, H, P], BF16, name="q_t")
-            nc.vector.tensor_copy(out=q_t[k][:], in_=ps_q[:])
+            nc.scalar.copy(out=q_t[k][:], in_=ps_q[:])
 
         def denominators(k):
             b = k // PAIRS_PER_BATCH
@@ -144,13 +154,21 @@ def tile_lineartransformerblock_pc_t_kernel(tc, q_feat, vk, k_sum, Wo_words, Wo_
                     start=True,
                     stop=True,
                 )
-            for h in range(H):
-                nc.scalar.activation(
-                    out=a_rows[k][:, x, :, 64 * h : 64 * h + 64],
-                    in_=ps_hs[:, h, :].rearrange("p (u w) -> p u w", u=2),
-                    func=COPY,
-                    scale=rden[k][:, x, h : h + 1],
+            if x == 0:
+                nc.vector.tensor_tensor(
+                    out=a_rows[k][:, x, :, :].rearrange("p u (h w) -> p h u w", h=H),
+                    in0=ps_hs[:].rearrange("p h (u w) -> p h u w", u=2),
+                    in1=rden[k][:, x, :].unsqueeze(2).unsqueeze(3).to_broadcast([P, H, 2, 64]),
+                    op=MULT,
                 )
+            else:
+                for h in range(H):
+                    nc.scalar.activation(
+                        out=a_rows[k][:, x, :, 64 * h : 64 * h + 64],
+                        in_=ps_hs[:, h, :].rearrange("p (u w) -> p u w", u=2),
+                        func=COPY,
+                        scale=rden[k][:, x, h : h + 1],
+                    )
 
         def transpose_a(k):
             ps_a = psum.tile([P, PAIR, 2, P], F32, tag="bank")
@@ -196,18 +214,18 @@ def tile_lineartransformerblock_pc_t_kernel(tc, q_feat, vk, k_sum, Wo_words, Wo_
                 in_=o_rows[:],
             )
 
-        transpose_k_sum()
-        transpose_vk(0)
         for r in range(PAIRS + LAG_PROJECT):
             if r < PAIRS:
                 transpose_q(r)
             if 0 <= r - LAG_TRANSPOSE_A < PAIRS:
                 transpose_a(r - LAG_TRANSPOSE_A)
-            if r < LAG_TRANSPOSE_A:
-                for b in range(1 + VK_PER_ROUND * r, min(B, 1 + VK_PER_ROUND * (r + 1))):
+            if r == 0:
+                transpose_k_sum()
+                transpose_vk(0)
+            if r >= FIRST_VK_ROUND:
+                first = 1 + VK_PER_ROUND * (r - FIRST_VK_ROUND)
+                for b in range(first, min(B, first + VK_PER_ROUND)):
                     transpose_vk(b)
-            if 0 <= r - LAG_QUANTISE < PAIRS:
-                quantise_a(r - LAG_QUANTISE)
             if 0 <= r - LAG_READ_OUT < PAIRS:
                 read_out(r - LAG_READ_OUT, 0)
             if 0 <= r - LAG_PROJECT < PAIRS:
@@ -217,3 +235,5 @@ def tile_lineartransformerblock_pc_t_kernel(tc, q_feat, vk, k_sum, Wo_words, Wo_
                 read_out(r - LAG_READ_OUT, 1)
             if 0 <= r - LAG_DENOMINATORS < PAIRS:
                 denominators(r - LAG_DENOMINATORS)
+            if 0 <= r - LAG_QUANTISE < PAIRS:
+                quantise_a(r - LAG_QUANTISE)

@@ -27,8 +27,8 @@ LAG_READ_OUT = 2
 LAG_TRANSPOSE_A = 4
 LAG_QUANTISE = 4
 LAG_PROJECT = 6
-VK_PER_ROUND = 2
-FIRST_VK_ROUND = 2
+LOADS_AHEAD = 3
+VK_LEAD = 3
 
 FLOPS = 2 * B * H * S * D * (D + 1) + 2 * B * S * E * C
 
@@ -44,15 +44,6 @@ def tile_lineartransformerblock_pc_t_kernel(tc, q_feat, vk, k_sum, Wo_words, Wo_
         psum = ctx.enter_context(tc.psum_pool(name="psum", bufs=7))
         ctx.enter_context(tc.manual_schedule())
 
-        ident_bf = consts.tile([P, P], BF16)
-        make_identity(nc, ident_bf[:])
-        ident_f32 = consts.tile([P, P], F32)
-        make_identity(nc, ident_f32[:])
-        perm_bf = consts.tile([P, P], BF16)
-        nc.vector.tensor_copy(
-            out=perm_bf[:].rearrange("p (u j e) -> p u j e", u=2, e=2),
-            in_=ident_bf[:].rearrange("p (j u e) -> p u j e", u=2, e=2),
-        )
         ks_rows = consts.tile([P, P], BF16)
         nc.vector.memset(ks_rows[:], 0.0)
         w_scales = consts.tile([P, C], U8, align_bytes=64)
@@ -71,12 +62,15 @@ def tile_lineartransformerblock_pc_t_kernel(tc, q_feat, vk, k_sum, Wo_words, Wo_
                 in_=q_feat[b].rearrange("h (p i) d -> p h i d", i=TILES)[:, :, first_tile : first_tile + tiles, :],
             )
 
+        def load_vk(b):
+            nc.sync.dma_start(out=vk_rows[:, H * b : H * b + H, :], in_=vk_view[:, H * b : H * b + H, :])
+
         load_q(0, 0, PAIR)
-        nc.sync.dma_start(out=vk_rows[:, 0:H, :], in_=vk_view[:, 0:H, :])
+        load_vk(0)
         nc.sync.dma_start(out=ks_rows[0 : B * H, :], in_=k_sum.rearrange("b h d -> (b h) d"))
         for g in range(1, PAIRS_PER_BATCH):
             load_q(0, PAIR * g, PAIR)
-        nc.sync.dma_start(out=vk_rows[:, H:, :], in_=vk_view[:, H:, :])
+        load_vk(1)
         w_codes = consts.tile([P, 4 * C], U8, align_bytes=64)
         nc.sync.dma_start(
             out=w_codes[:].bitcast(I32),
@@ -90,8 +84,19 @@ def tile_lineartransformerblock_pc_t_kernel(tc, q_feat, vk, k_sum, Wo_words, Wo_
         load_q(1, 0, TILES)
         bias = consts.tile([P, C], BF16)
         nc.sync.dma_start(out=bias[:], in_=bo.partition_broadcast(P))
-        for b in range(2, B):
+        for b in range(2, LOADS_AHEAD):
+            load_vk(b)
             load_q(b, 0, TILES)
+
+        ident_bf = consts.tile([P, P], BF16)
+        make_identity(nc, ident_bf[:])
+        ident_f32 = consts.tile([P, P], F32)
+        make_identity(nc, ident_f32[:])
+        perm_bf = consts.tile([P, P], BF16)
+        nc.vector.tensor_copy(
+            out=perm_bf[:].rearrange("p (u j e) -> p u j e", u=2, e=2),
+            in_=ident_bf[:].rearrange("p (j u e) -> p u j e", u=2, e=2),
+        )
 
         vk_t = consts.tile([P, B * H, D], BF16)
         ks_t = consts.tile([P, B * H], BF16)
@@ -122,7 +127,10 @@ def tile_lineartransformerblock_pc_t_kernel(tc, q_feat, vk, k_sum, Wo_words, Wo_
                 for h in range(H):
                     nc.tensor.transpose(ps_q[:, x, h, :], q_rows[b][:, h, PAIR * g + x, :], ident_bf[:])
             q_t[k] = work.tile([P, PAIR, H, P], BF16, name="q_t")
-            nc.scalar.copy(out=q_t[k][:], in_=ps_q[:])
+            nc.scalar.copy(
+                out=q_t[k][:].rearrange("p x h s -> p (x h s)").bitcast(F32),
+                in_=ps_q[:].rearrange("p x h s -> p (x h s)").bitcast(F32),
+            )
 
         def denominators(k):
             b = k // PAIRS_PER_BATCH
@@ -215,6 +223,9 @@ def tile_lineartransformerblock_pc_t_kernel(tc, q_feat, vk, k_sum, Wo_words, Wo_
             )
 
         for r in range(PAIRS + LAG_PROJECT):
+            if r % PAIRS_PER_BATCH == 0 and r // PAIRS_PER_BATCH + LOADS_AHEAD < B:
+                load_vk(r // PAIRS_PER_BATCH + LOADS_AHEAD)
+                load_q(r // PAIRS_PER_BATCH + LOADS_AHEAD, 0, TILES)
             if r < PAIRS:
                 transpose_q(r)
             if 0 <= r - LAG_TRANSPOSE_A < PAIRS:
@@ -222,10 +233,8 @@ def tile_lineartransformerblock_pc_t_kernel(tc, q_feat, vk, k_sum, Wo_words, Wo_
             if r == 0:
                 transpose_k_sum()
                 transpose_vk(0)
-            if r >= FIRST_VK_ROUND:
-                first = 1 + VK_PER_ROUND * (r - FIRST_VK_ROUND)
-                for b in range(first, min(B, first + VK_PER_ROUND)):
-                    transpose_vk(b)
+            if (r + VK_LEAD - LAG_READ_OUT) % PAIRS_PER_BATCH == 0 and 0 < (r + VK_LEAD - LAG_READ_OUT) // PAIRS_PER_BATCH < B:
+                transpose_vk((r + VK_LEAD - LAG_READ_OUT) // PAIRS_PER_BATCH)
             if 0 <= r - LAG_READ_OUT < PAIRS:
                 read_out(r - LAG_READ_OUT, 0)
             if 0 <= r - LAG_PROJECT < PAIRS:

@@ -27,6 +27,10 @@ LAG_READ_OUT = 2
 LAG_TRANSPOSE_A = 4
 LAG_QUANTISE = 4
 LAG_PROJECT = 6
+LAST_PAIRS_ON_SCALAR = 2
+WARM_UP_COLUMNS = 512
+WARM_UP_BEFORE_THE_FIRST_LOAD = 4
+WARM_UP_ROUNDS = 2
 LOADS_AHEAD = 3
 VK_LEAD = 3
 
@@ -43,6 +47,16 @@ def tile_lineartransformerblock_pc_t_kernel(tc, q_feat, vk, k_sum, Wo_words, Wo_
         ps_den_pool = ctx.enter_context(tc.psum_pool(name="ps_den_pool", bufs=1))
         psum = ctx.enter_context(tc.psum_pool(name="psum", bufs=7))
         ctx.enter_context(tc.manual_schedule())
+
+        warm_up = consts.tile([P, WARM_UP_COLUMNS], BF16)
+        nc.vector.memset(warm_up[:], 0.0)
+
+        def idle_matmuls(n):
+            ps_idle = psum.tile([P, WARM_UP_COLUMNS], F32, tag="bank")
+            for repeat in range(n):
+                nc.tensor.matmul(out=ps_idle[:], lhsT=warm_up[:, 0:P], rhs=warm_up[:], start=True, stop=True)
+
+        idle_matmuls(WARM_UP_BEFORE_THE_FIRST_LOAD)
 
         ks_rows = consts.tile([P, P], BF16)
         nc.vector.memset(ks_rows[:], 0.0)
@@ -162,7 +176,7 @@ def tile_lineartransformerblock_pc_t_kernel(tc, q_feat, vk, k_sum, Wo_words, Wo_
                     start=True,
                     stop=True,
                 )
-            if x == 0:
+            if x == 0 and k < PAIRS - LAST_PAIRS_ON_SCALAR:
                 nc.vector.tensor_tensor(
                     out=a_rows[k][:, x, :, :].rearrange("p u (h w) -> p h u w", h=H),
                     in0=ps_hs[:].rearrange("p h (u w) -> p h u w", u=2),
@@ -228,6 +242,8 @@ def tile_lineartransformerblock_pc_t_kernel(tc, q_feat, vk, k_sum, Wo_words, Wo_
                 load_q(r // PAIRS_PER_BATCH + LOADS_AHEAD, 0, TILES)
             if r < PAIRS:
                 transpose_q(r)
+            if r < WARM_UP_ROUNDS:
+                idle_matmuls(1)
             if 0 <= r - LAG_TRANSPOSE_A < PAIRS:
                 transpose_a(r - LAG_TRANSPOSE_A)
             if r == 0:

@@ -127,6 +127,7 @@ def tile_lineartransformerblock_pc_t_kernel(tc, q_feat, vk, k_sum, Wo_words, Wo_
             nc.vector.tensor_copy(out=vk_t[:, H * b : H * b + H, :], in_=ps_vk[:])
 
         q_t = {}
+        den = {}
         rden = {}
         a_rows = {}
         a_words = {}
@@ -158,10 +159,12 @@ def tile_lineartransformerblock_pc_t_kernel(tc, q_feat, vk, k_sum, Wo_words, Wo_
                         start=True,
                         stop=True,
                     )
-            den = work.tile([P, PAIR, H], F32, name="den")
-            nc.vector.tensor_scalar_add(out=den[:], in0=ps_den[:], scalar1=EPS)
+            den[k] = work.tile([P, PAIR, H], F32, name="den")
+            nc.vector.tensor_scalar_add(out=den[k][:], in0=ps_den[:], scalar1=EPS)
+
+        def reciprocals(k):
             rden[k] = work.tile([P, PAIR, H], F32, name="rden")
-            nc.vector.reciprocal(out=rden[k][:], in_=den[:])
+            nc.vector.reciprocal(out=rden[k][:], in_=den[k][:])
 
         def read_out(k, x):
             b = k // PAIRS_PER_BATCH
@@ -244,21 +247,23 @@ def tile_lineartransformerblock_pc_t_kernel(tc, q_feat, vk, k_sum, Wo_words, Wo_
                 transpose_q(r)
             if r < WARM_UP_ROUNDS:
                 idle_matmuls(1)
-            if 0 <= r - LAG_TRANSPOSE_A < PAIRS:
-                transpose_a(r - LAG_TRANSPOSE_A)
             if r == 0:
                 transpose_k_sum()
                 transpose_vk(0)
+            if 0 <= r - LAG_DENOMINATORS < PAIRS:
+                denominators(r - LAG_DENOMINATORS)
+            if 0 <= r - LAG_TRANSPOSE_A < PAIRS:
+                transpose_a(r - LAG_TRANSPOSE_A)
             if (r + VK_LEAD - LAG_READ_OUT) % PAIRS_PER_BATCH == 0 and 0 < (r + VK_LEAD - LAG_READ_OUT) // PAIRS_PER_BATCH < B:
                 transpose_vk((r + VK_LEAD - LAG_READ_OUT) // PAIRS_PER_BATCH)
             if 0 <= r - LAG_READ_OUT < PAIRS:
                 read_out(r - LAG_READ_OUT, 0)
+            if 0 <= r - LAG_DENOMINATORS < PAIRS:
+                reciprocals(r - LAG_DENOMINATORS)
             if 0 <= r - LAG_PROJECT < PAIRS:
                 project(r - LAG_PROJECT)
                 add_bias_and_store(r - LAG_PROJECT)
             if 0 <= r - LAG_READ_OUT < PAIRS:
                 read_out(r - LAG_READ_OUT, 1)
-            if 0 <= r - LAG_DENOMINATORS < PAIRS:
-                denominators(r - LAG_DENOMINATORS)
             if 0 <= r - LAG_QUANTISE < PAIRS:
                 quantise_a(r - LAG_QUANTISE)

@@ -28,6 +28,7 @@ LAG_TRANSPOSE_A = 4
 LAG_QUANTISE = 4
 LAG_PROJECT = 6
 LAST_PAIRS_ON_SCALAR = 2
+HEADS_ON_SCALAR = 3
 WARM_UP_COLUMNS = 512
 WARM_UP_BEFORE_THE_FIRST_LOAD = 4
 WARM_UP_ROUNDS = 2
@@ -187,12 +188,19 @@ def tile_lineartransformerblock_pc_t_kernel(tc, q_feat, vk, k_sum, Wo_words, Wo_
                     op=MULT,
                 )
             else:
-                for h in range(H):
+                heads_on_scalar = H if k >= PAIRS - LAST_PAIRS_ON_SCALAR else HEADS_ON_SCALAR
+                for h in range(heads_on_scalar):
                     nc.scalar.activation(
                         out=a_rows[k][:, x, :, 64 * h : 64 * h + 64],
                         in_=ps_hs[:, h, :].rearrange("p (u w) -> p u w", u=2),
                         func=COPY,
                         scale=rden[k][:, x, h : h + 1],
+                    )
+                for h in range(heads_on_scalar, H):
+                    nc.vector.tensor_scalar_mul(
+                        out=a_rows[k][:, x, :, 64 * h : 64 * h + 64],
+                        in0=ps_hs[:, h, :].rearrange("p (u w) -> p u w", u=2),
+                        scalar1=rden[k][:, x, h : h + 1],
                     )
 
         def transpose_a(k):

@@ -32,6 +32,7 @@ HEADS_ON_SCALAR = 3
 WARM_UP_COLUMNS = 512
 WARM_UP_BEFORE_THE_FIRST_LOAD = 4
 WARM_UP_ROUNDS = 2
+WARM_UP_IN_A_ROUND = 2
 LOADS_AHEAD = 3
 VK_LEAD = 3
 
@@ -254,7 +255,7 @@ def tile_lineartransformerblock_pc_t_kernel(tc, q_feat, vk, k_sum, Wo_words, Wo_
             if r < PAIRS:
                 transpose_q(r)
             if r < WARM_UP_ROUNDS:
-                idle_matmuls(1)
+                idle_matmuls(WARM_UP_IN_A_ROUND)
             if r == 0:
                 transpose_k_sum()
                 transpose_vk(0)

@@ -27,7 +27,7 @@ LAG_READ_OUT = 2
 LAG_TRANSPOSE_A = 4
 LAG_QUANTISE = 4
 LAG_PROJECT = 6
-LAST_PAIRS_ON_SCALAR = 2
+LAST_PAIRS = 3
 HEADS_ON_SCALAR = 3
 WARM_UP_COLUMNS = 512
 WARM_UP_BEFORE_THE_FIRST_LOAD = 4
@@ -72,16 +72,19 @@ def tile_lineartransformerblock_pc_t_kernel(tc, q_feat, vk, k_sum, Wo_words, Wo_
             q_b = q_pool.tile([P, H, TILES, D], BF16, name="q_b")
             q_rows.append(q_b)
 
-        def load_q(b, first_tile, tiles):
+        def load_q(b, first_tile, tiles, first_head=0, heads=H):
             nc.sync.dma_start(
-                out=q_rows[b][:, :, first_tile : first_tile + tiles, :],
-                in_=q_feat[b].rearrange("h (p i) d -> p h i d", i=TILES)[:, :, first_tile : first_tile + tiles, :],
+                out=q_rows[b][:, first_head : first_head + heads, first_tile : first_tile + tiles, :],
+                in_=q_feat[b].rearrange("h (p i) d -> p h i d", i=TILES)[
+                    :, first_head : first_head + heads, first_tile : first_tile + tiles, :
+                ],
             )
 
         def load_vk(b):
             nc.sync.dma_start(out=vk_rows[:, H * b : H * b + H, :], in_=vk_view[:, H * b : H * b + H, :])
 
-        load_q(0, 0, PAIR)
+        for first_head in range(0, H, 2):
+            load_q(0, 0, PAIR, first_head, 2)
         load_vk(0)
         nc.sync.dma_start(out=ks_rows[0 : B * H, :], in_=k_sum.rearrange("b h d -> (b h) d"))
         for g in range(1, PAIRS_PER_BATCH):
@@ -140,8 +143,8 @@ def tile_lineartransformerblock_pc_t_kernel(tc, q_feat, vk, k_sum, Wo_words, Wo_
         def transpose_q(k):
             b, g = divmod(k, PAIRS_PER_BATCH)
             ps_q = psum.tile([P, PAIR, H, P], BF16, tag="bank")
-            for x in range(PAIR):
-                for h in range(H):
+            for h in range(H):
+                for x in range(PAIR):
                     nc.tensor.transpose(ps_q[:, x, h, :], q_rows[b][:, h, PAIR * g + x, :], ident_bf[:])
             q_t[k] = work.tile([P, PAIR, H, P], BF16, name="q_t")
             nc.scalar.copy(
@@ -181,7 +184,7 @@ def tile_lineartransformerblock_pc_t_kernel(tc, q_feat, vk, k_sum, Wo_words, Wo_
                     start=True,
                     stop=True,
                 )
-            if x == 0 and k < PAIRS - LAST_PAIRS_ON_SCALAR:
+            if x == 0 and k < PAIRS - LAST_PAIRS:
                 nc.vector.tensor_tensor(
                     out=a_rows[k][:, x, :, :].rearrange("p u (h w) -> p h u w", h=H),
                     in0=ps_hs[:].rearrange("p h (u w) -> p h u w", u=2),
@@ -189,7 +192,7 @@ def tile_lineartransformerblock_pc_t_kernel(tc, q_feat, vk, k_sum, Wo_words, Wo_
                     op=MULT,
                 )
             else:
-                heads_on_scalar = H if k >= PAIRS - LAST_PAIRS_ON_SCALAR else HEADS_ON_SCALAR
+                heads_on_scalar = HEADS_ON_SCALAR if x == 1 else 2
                 for h in range(heads_on_scalar):
                     nc.scalar.activation(
                         out=a_rows[k][:, x, :, 64 * h : 64 * h + 64],
@@ -221,11 +224,17 @@ def tile_lineartransformerblock_pc_t_kernel(tc, q_feat, vk, k_sum, Wo_words, Wo_
                 in_=a_words[k][:].rearrange("p x s u -> p (x s u)").bitcast(BF16),
             )
 
+        def apart(k):
+            return k >= PAIRS - 1
+
         def project(k):
-            ps_out[k] = psum.tile([P, PAIR, C], F32, tag="bank", name="ps_o")
+            ps_out[k] = []
             for x in range(PAIR):
+                if x == 0 or apart(k):
+                    ps_o = psum.tile([P, PAIR, C], F32, tag="bank", name="ps_o")
+                ps_out[k].append(ps_o)
                 nc.tensor.matmul_mx(
-                    out=ps_out[k][:, x, :],
+                    out=ps_o[:, x, :],
                     lhsT=a_codes[k][:, P * x : P * x + P].bitcast(FP8X4),
                     lhsT_scale=a_scales[k][:, P * x : P * x + P],
                     rhs=w_codes[:].bitcast(FP8X4),
@@ -237,16 +246,16 @@ def tile_lineartransformerblock_pc_t_kernel(tc, q_feat, vk, k_sum, Wo_words, Wo_
         def add_bias_and_store(k):
             b, g = divmod(k, PAIRS_PER_BATCH)
             o_rows = out_pool.tile([P, PAIR, C], F32, name="o_rows")
-            nc.vector.tensor_tensor(
-                out=o_rows[:],
-                in0=ps_out[k][:],
-                in1=bias[:].unsqueeze(1).to_broadcast([P, PAIR, C]),
-                op=ADD,
-            )
-            nc.sync.dma_start(
-                out=out[b].rearrange("(p i) c -> p i c", i=TILES)[:, PAIR * g : PAIR * g + PAIR, :],
-                in_=o_rows[:],
-            )
+            out_rows = out[b].rearrange("(p i) c -> p i c", i=TILES)[:, PAIR * g : PAIR * g + PAIR, :]
+            tiles = 1 if apart(k) else PAIR
+            for x in range(0, PAIR, tiles):
+                nc.vector.tensor_tensor(
+                    out=o_rows[:, x : x + tiles, :],
+                    in0=ps_out[k][x][:, x : x + tiles, :],
+                    in1=bias[:].unsqueeze(1).to_broadcast([P, tiles, C]),
+                    op=ADD,
+                )
+                nc.sync.dma_start(out=out_rows[:, x : x + tiles, :], in_=o_rows[:, x : x + tiles, :])
 
         for r in range(PAIRS + LAG_PROJECT):
             if r % PAIRS_PER_BATCH == 0 and r // PAIRS_PER_BATCH + LOADS_AHEAD < B:

@@ -27,8 +27,6 @@ LAG_READ_OUT = 2
 LAG_TRANSPOSE_A = 4
 LAG_QUANTISE = 4
 LAG_PROJECT = 6
-LAST_PAIRS = 3
-HEADS_ON_SCALAR = 3
 WARM_UP_COLUMNS = 512
 WARM_UP_BEFORE_THE_FIRST_LOAD = 4
 WARM_UP_ROUNDS = 2
@@ -184,7 +182,7 @@ def tile_lineartransformerblock_pc_t_kernel(tc, q_feat, vk, k_sum, Wo_words, Wo_
                     start=True,
                     stop=True,
                 )
-            if x == 0 and k < PAIRS - LAST_PAIRS:
+            if x == 0 or k % 4 == 1:
                 nc.vector.tensor_tensor(
                     out=a_rows[k][:, x, :, :].rearrange("p u (h w) -> p h u w", h=H),
                     in0=ps_hs[:].rearrange("p h (u w) -> p h u w", u=2),
@@ -192,19 +190,12 @@ def tile_lineartransformerblock_pc_t_kernel(tc, q_feat, vk, k_sum, Wo_words, Wo_
                     op=MULT,
                 )
             else:
-                heads_on_scalar = HEADS_ON_SCALAR if x == 1 else 2
-                for h in range(heads_on_scalar):
+                for h in range(H):
                     nc.scalar.activation(
                         out=a_rows[k][:, x, :, 64 * h : 64 * h + 64],
                         in_=ps_hs[:, h, :].rearrange("p (u w) -> p u w", u=2),
                         func=COPY,
                         scale=rden[k][:, x, h : h + 1],
-                    )
-                for h in range(heads_on_scalar, H):
-                    nc.vector.tensor_scalar_mul(
-                        out=a_rows[k][:, x, :, 64 * h : 64 * h + 64],
-                        in0=ps_hs[:, h, :].rearrange("p (u w) -> p u w", u=2),
-                        scalar1=rden[k][:, x, h : h + 1],
                     )
 
         def transpose_a(k):

@@ -129,6 +129,8 @@ def tile_lineartransformerblock_pc_t_kernel(tc, q_feat, vk, k_sum, Wo_words, Wo_
                 nc.tensor.transpose(ps_vk[:, h, :], vk_rows[:, H * b + h, :], perm_bf[:])
             nc.vector.tensor_copy(out=vk_t[:, H * b : H * b + H, :], in_=ps_vk[:])
 
+        ps_q = {}
+        ps_hs = {}
         q_t = {}
         den = {}
         rden = {}
@@ -138,16 +140,19 @@ def tile_lineartransformerblock_pc_t_kernel(tc, q_feat, vk, k_sum, Wo_words, Wo_
         a_scales = {}
         ps_out = {}
 
-        def transpose_q(k):
+        def transpose_q(k, heads):
             b, g = divmod(k, PAIRS_PER_BATCH)
-            ps_q = psum.tile([P, PAIR, H, P], BF16, tag="bank")
-            for h in range(H):
+            if heads[0] == 0:
+                ps_q[k] = psum.tile([P, PAIR, H, P], BF16, tag="bank", name="ps_q_k")
+            for h in heads:
                 for x in range(PAIR):
-                    nc.tensor.transpose(ps_q[:, x, h, :], q_rows[b][:, h, PAIR * g + x, :], ident_bf[:])
+                    nc.tensor.transpose(ps_q[k][:, x, h, :], q_rows[b][:, h, PAIR * g + x, :], ident_bf[:])
+
+        def copy_q(k):
             q_t[k] = work.tile([P, PAIR, H, P], BF16, name="q_t")
             nc.scalar.copy(
                 out=q_t[k][:].rearrange("p x h s -> p (x h s)").bitcast(F32),
-                in_=ps_q[:].rearrange("p x h s -> p (x h s)").bitcast(F32),
+                in_=ps_q[k][:].rearrange("p x h s -> p (x h s)").bitcast(F32),
             )
 
         def denominators(k):
@@ -169,23 +174,26 @@ def tile_lineartransformerblock_pc_t_kernel(tc, q_feat, vk, k_sum, Wo_words, Wo_
             rden[k] = work.tile([P, PAIR, H], F32, name="rden")
             nc.vector.reciprocal(out=rden[k][:], in_=den[k][:])
 
-        def read_out(k, x):
+        def read_out_heads(k, x, heads):
             b = k // PAIRS_PER_BATCH
-            if x == 0:
-                a_rows[k] = work.tile([P, PAIR, 2, E // 2], BF16, name="a_rows")
-            ps_hs = psum.tile([P, H, D], F32, tag="bank")
-            for h in range(H):
+            if heads[0] == 0:
+                ps_hs[k, x] = psum.tile([P, H, D], F32, tag="bank", name="ps_hs_kx")
+            for h in heads:
                 nc.tensor.matmul(
-                    out=ps_hs[:, h, :],
+                    out=ps_hs[k, x][:, h, :],
                     lhsT=q_t[k][:, x, h, :],
                     rhs=vk_t[:, H * b + h, :],
                     start=True,
                     stop=True,
                 )
-            if x == 0 or k % 4 == 1:
+
+        def normalise(k, x):
+            if x == 0:
+                a_rows[k] = work.tile([P, PAIR, 2, E // 2], BF16, name="a_rows")
+            if x == 0 or k % 16 == 1:
                 nc.vector.tensor_tensor(
                     out=a_rows[k][:, x, :, :].rearrange("p u (h w) -> p h u w", h=H),
-                    in0=ps_hs[:].rearrange("p h (u w) -> p h u w", u=2),
+                    in0=ps_hs[k, x][:].rearrange("p h (u w) -> p h u w", u=2),
                     in1=rden[k][:, x, :].unsqueeze(2).unsqueeze(3).to_broadcast([P, H, 2, 64]),
                     op=MULT,
                 )
@@ -193,7 +201,7 @@ def tile_lineartransformerblock_pc_t_kernel(tc, q_feat, vk, k_sum, Wo_words, Wo_
                 for h in range(H):
                     nc.scalar.activation(
                         out=a_rows[k][:, x, :, 64 * h : 64 * h + 64],
-                        in_=ps_hs[:, h, :].rearrange("p (u w) -> p u w", u=2),
+                        in_=ps_hs[k, x][:, h, :].rearrange("p (u w) -> p u w", u=2),
                         func=COPY,
                         scale=rden[k][:, x, h : h + 1],
                     )
@@ -253,7 +261,13 @@ def tile_lineartransformerblock_pc_t_kernel(tc, q_feat, vk, k_sum, Wo_words, Wo_
                 load_vk(r // PAIRS_PER_BATCH + LOADS_AHEAD)
                 load_q(r // PAIRS_PER_BATCH + LOADS_AHEAD, 0, TILES)
             if r < PAIRS:
-                transpose_q(r)
+                transpose_q(r, (0, 1))
+            if 0 <= r - LAG_READ_OUT < PAIRS:
+                read_out_heads(r - LAG_READ_OUT, 0, (0, 1, 2, 3))
+                normalise(r - LAG_READ_OUT, 0)
+            if r < PAIRS:
+                transpose_q(r, (2, 3))
+                copy_q(r)
             if r < WARM_UP_ROUNDS:
                 idle_matmuls(WARM_UP_IN_A_ROUND)
             if r == 0:
@@ -266,13 +280,14 @@ def tile_lineartransformerblock_pc_t_kernel(tc, q_feat, vk, k_sum, Wo_words, Wo_
             if (r + VK_LEAD - LAG_READ_OUT) % PAIRS_PER_BATCH == 0 and 0 < (r + VK_LEAD - LAG_READ_OUT) // PAIRS_PER_BATCH < B:
                 transpose_vk((r + VK_LEAD - LAG_READ_OUT) // PAIRS_PER_BATCH)
             if 0 <= r - LAG_READ_OUT < PAIRS:
-                read_out(r - LAG_READ_OUT, 0)
-            if 0 <= r - LAG_DENOMINATORS < PAIRS:
-                reciprocals(r - LAG_DENOMINATORS)
+                read_out_heads(r - LAG_READ_OUT, 1, (0, 1))
             if 0 <= r - LAG_PROJECT < PAIRS:
                 project(r - LAG_PROJECT)
                 add_bias_and_store(r - LAG_PROJECT)
+            if 0 <= r - LAG_DENOMINATORS < PAIRS:
+                reciprocals(r - LAG_DENOMINATORS)
             if 0 <= r - LAG_READ_OUT < PAIRS:
-                read_out(r - LAG_READ_OUT, 1)
+                read_out_heads(r - LAG_READ_OUT, 1, (2, 3))
+                normalise(r - LAG_READ_OUT, 1)
             if 0 <= r - LAG_QUANTISE < PAIRS:
                 quantise_a(r - LAG_QUANTISE)

from contextlib import ExitStack

import concourse.mybir as mybir
from concourse.masks import make_identity

BF16 = mybir.dt.bfloat16
F32 = mybir.dt.float32
I32 = mybir.dt.int32
U32 = mybir.dt.uint32
U8 = mybir.dt.uint8
FP8X4 = mybir.dt.float8_e4m3fn_x4
COPY = mybir.ActivationFunctionType.Copy
ADD = mybir.AluOpType.add
MULT = mybir.AluOpType.mult

B, H, S, D, C = 8, 4, 1024, 128, 256
E = H * D
P = 128
EPS = 1e-15
TILES = S // P
PAIR = 2
PAIRS = B * TILES // PAIR
PAIRS_PER_BATCH = TILES // PAIR

LAG_DENOMINATORS = 1
LAG_READ_OUT = 2
LAG_TRANSPOSE_A = 4
LAG_QUANTISE = 4
LAG_PROJECT = 6
WARM_UP_COLUMNS = 512
WARM_UP_BEFORE_THE_FIRST_LOAD = 4
WARM_UP_ROUNDS = 2
WARM_UP_IN_A_ROUND = 2
LOADS_AHEAD = 3
VK_LEAD = 3

FLOPS = 2 * B * H * S * D * (D + 1) + 2 * B * S * E * C


def tile_lineartransformerblock_pc_t_kernel(tc, q_feat, vk, k_sum, Wo_words, Wo_scales, bo, out):
    nc = tc.nc
    with ExitStack() as ctx:
        consts = ctx.enter_context(tc.tile_pool(name="consts", bufs=1))
        q_pool = ctx.enter_context(tc.tile_pool(name="q_pool", bufs=B))
        work = ctx.enter_context(tc.tile_pool(name="work", bufs=4))
        out_pool = ctx.enter_context(tc.tile_pool(name="out_pool", bufs=4))
        ps_den_pool = ctx.enter_context(tc.psum_pool(name="ps_den_pool", bufs=1))
        psum = ctx.enter_context(tc.psum_pool(name="psum", bufs=7))
        ctx.enter_context(tc.manual_schedule())

        warm_up = consts.tile([P, WARM_UP_COLUMNS], BF16)
        nc.vector.memset(warm_up[:], 0.0)

        def idle_matmuls(n):
            ps_idle = psum.tile([P, WARM_UP_COLUMNS], F32, tag="bank")
            for repeat in range(n):
                nc.tensor.matmul(out=ps_idle[:], lhsT=warm_up[:, 0:P], rhs=warm_up[:], start=True, stop=True)

        idle_matmuls(WARM_UP_BEFORE_THE_FIRST_LOAD)

        ks_rows = consts.tile([P, P], BF16)
        nc.vector.memset(ks_rows[:], 0.0)
        w_scales = consts.tile([P, C], U8, align_bytes=64)
        nc.vector.memset(w_scales[:].bitcast(I32), 0)

        vk_rows = consts.tile([P, B * H, D], BF16)
        vk_view = vk.rearrange("b h n d -> n (b h) d")
        q_rows = []
        for b in range(B):
            q_b = q_pool.tile([P, H, TILES, D], BF16, name="q_b")
            q_rows.append(q_b)

        def load_q(b, first_tile, tiles, first_head=0, heads=H):
            nc.sync.dma_start(
                out=q_rows[b][:, first_head : first_head + heads, first_tile : first_tile + tiles, :],
                in_=q_feat[b].rearrange("h (p i) d -> p h i d", i=TILES)[
                    :, first_head : first_head + heads, first_tile : first_tile + tiles, :
                ],
            )

        def load_vk(b):
            nc.sync.dma_start(out=vk_rows[:, H * b : H * b + H, :], in_=vk_view[:, H * b : H * b + H, :])

        for first_head in range(0, H, 2):
            load_q(0, 0, PAIR, first_head, 2)
        load_vk(0)
        nc.sync.dma_start(out=ks_rows[0 : B * H, :], in_=k_sum.rearrange("b h d -> (b h) d"))
        for g in range(1, PAIRS_PER_BATCH):
            load_q(0, PAIR * g, PAIR)
        load_vk(1)
        w_codes = consts.tile([P, 4 * C], U8, align_bytes=64)
        nc.sync.dma_start(
            out=w_codes[:].bitcast(I32),
            in_=Wo_words[0].rearrange("p n t -> p (n t)").bitcast(I32),
        )
        for quad in range(4):
            nc.sync.dma_start(
                out=w_scales[32 * quad : 32 * quad + 4, :].bitcast(I32),
                in_=Wo_scales[0, 4 * quad : 4 * quad + 4, :].bitcast(I32),
            )
        load_q(1, 0, TILES)
        bias = consts.tile([P, C], BF16)
        nc.sync.dma_start(out=bias[:], in_=bo.partition_broadcast(P))
        for b in range(2, LOADS_AHEAD):
            load_vk(b)
            load_q(b, 0, TILES)

        ident_bf = consts.tile([P, P], BF16)
        make_identity(nc, ident_bf[:])
        ident_f32 = consts.tile([P, P], F32)
        make_identity(nc, ident_f32[:])
        perm_bf = consts.tile([P, P], BF16)
        nc.vector.tensor_copy(
            out=perm_bf[:].rearrange("p (u j e) -> p u j e", u=2, e=2),
            in_=ident_bf[:].rearrange("p (j u e) -> p u j e", u=2, e=2),
        )

        vk_t = consts.tile([P, B * H, D], BF16)
        ks_t = consts.tile([P, B * H], BF16)

        def transpose_k_sum():
            ps_ks = psum.tile([P, H, P], BF16, tag="bank")
            nc.tensor.transpose(ps_ks[:, 0, :], ks_rows[:], ident_bf[:])
            nc.vector.tensor_copy(out=ks_t[:], in_=ps_ks[:, 0, 0 : B * H])

        def transpose_vk(b):
            ps_vk = psum.tile([P, H, P], BF16, tag="bank")
            for h in range(H):
                nc.tensor.transpose(ps_vk[:, h, :], vk_rows[:, H * b + h, :], perm_bf[:])
            nc.vector.tensor_copy(out=vk_t[:, H * b : H * b + H, :], in_=ps_vk[:])

        ps_q = {}
        ps_hs = {}
        q_t = {}
        den = {}
        rden = {}
        a_rows = {}
        a_words = {}
        a_codes = {}
        a_scales = {}
        ps_out = {}

        def transpose_q(k, heads):
            b, g = divmod(k, PAIRS_PER_BATCH)
            if heads[0] == 0:
                ps_q[k] = psum.tile([P, PAIR, H, P], BF16, tag="bank", name="ps_q_k")
            for h in heads:
                for x in range(PAIR):
                    nc.tensor.transpose(ps_q[k][:, x, h, :], q_rows[b][:, h, PAIR * g + x, :], ident_bf[:])

        def copy_q(k):
            q_t[k] = work.tile([P, PAIR, H, P], BF16, name="q_t")
            nc.scalar.copy(
                out=q_t[k][:].rearrange("p x h s -> p (x h s)").bitcast(F32),
                in_=ps_q[k][:].rearrange("p x h s -> p (x h s)").bitcast(F32),
            )

        def denominators(k):
            b = k // PAIRS_PER_BATCH
            ps_den = ps_den_pool.tile([P, PAIR, H], F32)
            for x in range(PAIR):
                for h in range(H):
                    nc.tensor.matmul(
                        out=ps_den[:, x, h : h + 1],
                        lhsT=q_t[k][:, x, h, :],
                        rhs=ks_t[:, H * b + h : H * b + h + 1],
                        start=True,
                        stop=True,
                    )
            den[k] = work.tile([P, PAIR, H], F32, name="den")
            nc.vector.tensor_scalar_add(out=den[k][:], in0=ps_den[:], scalar1=EPS)

        def reciprocals(k):
            rden[k] = work.tile([P, PAIR, H], F32, name="rden")
            nc.vector.reciprocal(out=rden[k][:], in_=den[k][:])

        def read_out_heads(k, x, heads):
            b = k // PAIRS_PER_BATCH
            if heads[0] == 0:
                ps_hs[k, x] = psum.tile([P, H, D], F32, tag="bank", name="ps_hs_kx")
            for h in heads:
                nc.tensor.matmul(
                    out=ps_hs[k, x][:, h, :],
                    lhsT=q_t[k][:, x, h, :],
                    rhs=vk_t[:, H * b + h, :],
                    start=True,
                    stop=True,
                )

        def normalise(k, x):
            if x == 0:
                a_rows[k] = work.tile([P, PAIR, 2, E // 2], BF16, name="a_rows")
            if x == 0 or k % 16 == 1:
                nc.vector.tensor_tensor(
                    out=a_rows[k][:, x, :, :].rearrange("p u (h w) -> p h u w", h=H),
                    in0=ps_hs[k, x][:].rearrange("p h (u w) -> p h u w", u=2),
                    in1=rden[k][:, x, :].unsqueeze(2).unsqueeze(3).to_broadcast([P, H, 2, 64]),
                    op=MULT,
                )
            else:
                for h in range(H):
                    nc.scalar.activation(
                        out=a_rows[k][:, x, :, 64 * h : 64 * h + 64],
                        in_=ps_hs[k, x][:, h, :].rearrange("p (u w) -> p u w", u=2),
                        func=COPY,
                        scale=rden[k][:, x, h : h + 1],
                    )

        def transpose_a(k):
            ps_a = psum.tile([P, PAIR, 2, P], F32, tag="bank")
            for x in range(PAIR):
                for u in range(2):
                    nc.tensor.transpose(ps_a[:, x, u, :], a_rows[k][:, x, u, :].bitcast(F32), ident_f32[:])
            a_words[k] = work.tile([P, PAIR, P, 2], F32, name="a_words", align_bytes=64)
            nc.scalar.copy(out=a_words[k][:], in_=ps_a[:].rearrange("p x u s -> p x s u"))

        def quantise_a(k):
            a_codes[k] = work.tile([P, PAIR * P], U32, name="a_codes", align_bytes=64)
            a_scales[k] = work.tile([P, PAIR * P], U8, name="a_scales", align_bytes=64)
            nc.vector.quantize_mx(
                out=a_codes[k][:].bitcast(FP8X4),
                scales=a_scales[k][:],
                in_=a_words[k][:].rearrange("p x s u -> p (x s u)").bitcast(BF16),
            )

        def apart(k):
            return k >= PAIRS - 1

        def project(k):
            ps_out[k] = []
            for x in range(PAIR):
                if x == 0 or apart(k):
                    ps_o = psum.tile([P, PAIR, C], F32, tag="bank", name="ps_o")
                ps_out[k].append(ps_o)
                nc.tensor.matmul_mx(
                    out=ps_o[:, x, :],
                    lhsT=a_codes[k][:, P * x : P * x + P].bitcast(FP8X4),
                    lhsT_scale=a_scales[k][:, P * x : P * x + P],
                    rhs=w_codes[:].bitcast(FP8X4),
                    rhs_scale=w_scales[:],
                    start=True,
                    stop=True,
                )

        def add_bias_and_store(k):
            b, g = divmod(k, PAIRS_PER_BATCH)
            o_rows = out_pool.tile([P, PAIR, C], F32, name="o_rows")
            out_rows = out[b].rearrange("(p i) c -> p i c", i=TILES)[:, PAIR * g : PAIR * g + PAIR, :]
            tiles = 1 if apart(k) else PAIR
            for x in range(0, PAIR, tiles):
                nc.vector.tensor_tensor(
                    out=o_rows[:, x : x + tiles, :],
                    in0=ps_out[k][x][:, x : x + tiles, :],
                    in1=bias[:].unsqueeze(1).to_broadcast([P, tiles, C]),
                    op=ADD,
                )
                nc.sync.dma_start(out=out_rows[:, x : x + tiles, :], in_=o_rows[:, x : x + tiles, :])

        for r in range(PAIRS + LAG_PROJECT):
            if r % PAIRS_PER_BATCH == 0 and r // PAIRS_PER_BATCH + LOADS_AHEAD < B:
                load_vk(r // PAIRS_PER_BATCH + LOADS_AHEAD)
                load_q(r // PAIRS_PER_BATCH + LOADS_AHEAD, 0, TILES)
            if r < PAIRS:
                transpose_q(r, (0, 1))
            if 0 <= r - LAG_READ_OUT < PAIRS:
                read_out_heads(r - LAG_READ_OUT, 0, (0, 1, 2, 3))
                normalise(r - LAG_READ_OUT, 0)
            if r < PAIRS:
                transpose_q(r, (2, 3))
                copy_q(r)
            if r < WARM_UP_ROUNDS:
                idle_matmuls(WARM_UP_IN_A_ROUND)
            if r == 0:
                transpose_k_sum()
                transpose_vk(0)
            if 0 <= r - LAG_DENOMINATORS < PAIRS:
                denominators(r - LAG_DENOMINATORS)
            if 0 <= r - LAG_TRANSPOSE_A < PAIRS:
                transpose_a(r - LAG_TRANSPOSE_A)
            if (r + VK_LEAD - LAG_READ_OUT) % PAIRS_PER_BATCH == 0 and 0 < (r + VK_LEAD - LAG_READ_OUT) // PAIRS_PER_BATCH < B:
                transpose_vk((r + VK_LEAD - LAG_READ_OUT) // PAIRS_PER_BATCH)
            if 0 <= r - LAG_READ_OUT < PAIRS:
                read_out_heads(r - LAG_READ_OUT, 1, (0, 1))
            if 0 <= r - LAG_PROJECT < PAIRS:
                project(r - LAG_PROJECT)
                add_bias_and_store(r - LAG_PROJECT)
            if 0 <= r - LAG_DENOMINATORS < PAIRS:
                reciprocals(r - LAG_DENOMINATORS)
            if 0 <= r - LAG_READ_OUT < PAIRS:
                read_out_heads(r - LAG_READ_OUT, 1, (2, 3))
                normalise(r - LAG_READ_OUT, 1)
            if 0 <= r - LAG_QUANTISE < PAIRS:
                quantise_a(r - LAG_QUANTISE)
